import numpy as np
import ml_dtypes


def mxq(x, axis, fmt="e4m3"):
    dtype, down = {"e4m3": (ml_dtypes.float8_e4m3fn, 7), "e5m2": (ml_dtypes.float8_e5m2, 14)}[fmt]
    v = np.moveaxis(np.asarray(x, np.float32).astype(ml_dtypes.bfloat16).astype(np.float64), axis, -1)
    blocks = v.reshape(v.shape[:-1] + (-1, 32))
    amax = np.abs(blocks).max(-1, keepdims=True)
    byte = np.maximum(np.where(amax > 0, np.frexp(amax)[1] - 1 + 127, 0) - down, 1)
    scale = np.exp2(byte - 127.0)
    codes = (blocks / scale).astype(np.float32).astype(dtype).astype(np.float64)
    return np.moveaxis((codes * scale).reshape(v.shape), -1, axis)


WIDE = False


def mx_kscale(k):
    if not WIDE:
        return np.ones(k)
    levels = np.array([20, -20, 10, -10, 0])
    a = np.random.permutation(np.resize(levels, k // 512 * 4)).reshape(k // 512, 4)
    idx = np.arange(k)
    return np.exp2(a[idx // 512, idx % 128 // 32])


BF16 = ml_dtypes.bfloat16


def bf(x):
    return np.asarray(x, np.float32).astype(BF16)


def f64(x):
    return np.asarray(x).astype(np.float64)


B, L, H = 2, 256, 512
HH = H // 2
T = B * L
BASE = 10000.0


def rope_tables():
    inv_freq = 1.0 / BASE ** (np.arange(0, H, 2) / H)
    freqs = np.outer(np.arange(L), inv_freq)
    emb = np.concatenate([freqs, freqs], axis=-1)
    return np.cos(emb), np.sin(emb)


def rotate_half(x):
    x1, x2 = np.split(x, 2, axis=-1)
    return np.concatenate([-x2, x1], axis=-1)


def setup_inputs():
    s = mx_kscale(T).reshape(B, L, 1)
    cos, sin = rope_tables()
    x = np.random.standard_normal((B, L, H)) * 0.2 * s
    w = np.random.standard_normal((H, H)) * 0.5 / np.sqrt(H)
    g = np.random.standard_normal((B, L, H)) * np.exp2(np.random.randint(-12, 1, (B, L, 1))) / s
    return {"hidden_states": bf(x), "W_q": bf(w), "cos": bf(cos), "sin": bf(sin), "grad_out": bf(g)}


def reference(hidden_states, W_q, cos, sin, grad_out):
    x = f64(hidden_states)
    h = x * f64(cos)[None, :, :] + rotate_half(x) * f64(sin)[None, :, :]
    h2 = h.reshape(T, H)
    g2 = f64(grad_out).reshape(T, H)
    return mxq(g2, 0, "e5m2").T @ mxq(h2, 0, "e4m3")

@@ -1,0 +1,140 @@
+from contextlib import ExitStack
+
+import concourse.mybir as mybir
+
+BF16 = mybir.dt.bfloat16
+F32 = mybir.dt.float32
+U32 = mybir.dt.uint32
+U8 = mybir.dt.uint8
+E4M3_X4 = mybir.dt.float8_e4m3fn_x4
+E5M2_X4 = mybir.dt.float8_e5m2_x4
+ALU = mybir.AluOpType
+
+P = 128
+PACK = 4
+BATCH = 2
+LENGTH = 256
+WIDTH = 512
+HALF = WIDTH // 2
+ROWS = LENGTH // P
+CHUNK = 128
+CHUNKS = WIDTH // CHUNK
+
+FLOPS = 2 * BATCH * LENGTH * WIDTH * WIDTH
+BYTES = 2 * (2 * BATCH * LENGTH * WIDTH + 2 * LENGTH * WIDTH) + 4 * WIDTH * WIDTH
+
+
+def tile_denseattentiononehead_pa_s_kernel(tc, hidden_states, W_q, cos, sin, grad_out, out):
+    nc = tc.nc
+
+    x_rows = hidden_states.rearrange("b (p i) w -> b i p w", i=ROWS)
+    cos_rows = cos.rearrange("(p i) w -> i p w", i=ROWS)
+    sin_rows = sin.rearrange("(p i) w -> i p w", i=ROWS)
+    g_rows = grad_out.rearrange("b (p i) o -> b p i o", i=ROWS)
+
+    with ExitStack() as ctx:
+        keep = ctx.enter_context(tc.tile_pool(name="keep", bufs=1))
+        results = ctx.enter_context(tc.tile_pool(name="results", bufs=CHUNKS))
+        psum = ctx.enter_context(tc.psum_pool(name="psum", bufs=CHUNKS))
+        ctx.enter_context(tc.manual_schedule())
+
+        x_sb = keep.tile([P, PACK, WIDTH], BF16)
+        cos_sb = keep.tile([P, ROWS, WIDTH], BF16)
+        sin_sb = keep.tile([P, ROWS, WIDTH], BF16)
+        g_sb = keep.tile([P, PACK, WIDTH], BF16)
+
+        for i in range(ROWS):
+            for b in range(BATCH):
+                nc.sync.dma_start(out=x_sb[:, b * ROWS + i, :], in_=x_rows[b, i, :, :])
+                if b == 0:
+                    nc.sync.dma_start(out=cos_sb[:, i, :], in_=cos_rows[i, :, :])
+                    nc.sync.dma_start(out=sin_sb[:, i, :], in_=sin_rows[i, :, :])
+        for b in range(BATCH):
+            nc.sync.dma_start(out=g_sb[:, b * ROWS : (b + 1) * ROWS, :], in_=g_rows[b, :, :, :])
+
+        x_cos = keep.tile([P, PACK, WIDTH], F32)
+        x_sin_hi = keep.tile([P, PACK, HALF], F32)
+        x_sin_lo = keep.tile([P, PACK, HALF], F32)
+        for i in range(ROWS):
+            for b in range(BATCH):
+                t = b * ROWS + i
+                nc.vector.tensor_tensor(
+                    out=x_cos[:, t, :], in0=x_sb[:, t, :], in1=cos_sb[:, i, :], op=ALU.mult
+                )
+                nc.vector.tensor_tensor(
+                    out=x_sin_hi[:, t, :], in0=x_sb[:, t, :HALF], in1=sin_sb[:, i, HALF:], op=ALU.mult
+                )
+                nc.vector.tensor_tensor(
+                    out=x_sin_lo[:, t, :], in0=x_sb[:, t, HALF:], in1=sin_sb[:, i, :HALF], op=ALU.mult
+                )
+
+        g_grouped = keep.tile([P, WIDTH, PACK], BF16, align_bytes=64)
+        for c in range(CHUNKS):
+            cols = slice(c * CHUNK, (c + 1) * CHUNK)
+            nc.scalar.copy(out=g_grouped[:, cols, :], in_=g_sb[:, :, cols].rearrange("p t o -> p o t"))
+
+        g_codes = keep.tile([P, WIDTH], U32, align_bytes=64)
+        g_scales = keep.tile([P, WIDTH], U8, align_bytes=64)
+
+        def quantise_g(c):
+            cols = slice(c * CHUNK, (c + 1) * CHUNK)
+            nc.vector.quantize_mx(
+                out=g_codes[:, cols].bitcast(E5M2_X4),
+                scales=g_scales[:, cols],
+                in_=g_grouped[:, cols, :].rearrange("p o t -> p (o t)"),
+            )
+
+        h_grouped = keep.tile([P, WIDTH, PACK], BF16, align_bytes=64)
+        h_codes = keep.tile([P, WIDTH], U32, align_bytes=64)
+        h_scales = keep.tile([P, WIDTH], U8, align_bytes=64)
+
+        def rotate(c):
+            cols = slice(c * CHUNK, (c + 1) * CHUNK)
+            if c * CHUNK >= HALF:
+                x_sin, op = x_sin_hi, ALU.add
+            else:
+                x_sin, op = x_sin_lo, ALU.subtract
+            half_cols = slice(c * CHUNK % HALF, c * CHUNK % HALF + CHUNK)
+            nc.vector.tensor_tensor(
+                out=h_grouped[:, cols, :],
+                in0=x_cos[:, :, cols].rearrange("p t j -> p j t"),
+                in1=x_sin[:, :, half_cols].rearrange("p t j -> p j t"),
+                op=op,
+            )
+
+        def quantise_h(c):
+            cols = slice(c * CHUNK, (c + 1) * CHUNK)
+            nc.vector.quantize_mx(
+                out=h_codes[:, cols].bitcast(E4M3_X4),
+                scales=h_scales[:, cols],
+                in_=h_grouped[:, cols, :].rearrange("p j t -> p (j t)"),
+            )
+
+        order = list(range(CHUNKS // 2, CHUNKS)) + list(range(CHUNKS // 2))
+        rotate(order[0])
+        for n in range(1, CHUNKS):
+            rotate(order[n])
+            quantise_h(order[n - 1])
+        quantise_g(0)
+        quantise_h(order[CHUNKS - 1])
+        for c in range(1, CHUNKS):
+            quantise_g(c)
+
+        for c in range(CHUNKS):
+            cols = slice(c * CHUNK, (c + 1) * CHUNK)
+            acc = psum.tile([CHUNK, WIDTH], F32)
+            nc.tensor.matmul_mx(
+                out=acc[:],
+                lhsT=g_codes[:, cols].bitcast(E5M2_X4),
+                lhsT_scale=g_scales[:, cols],
+                rhs=h_codes[:].bitcast(E4M3_X4),
+                rhs_scale=h_scales[:],
+                start=True,
+                stop=True,
+            )
+            result = results.tile([CHUNK, WIDTH], F32)
+            if c % 2 == 0:
+                nc.scalar.copy(out=result[:], in_=acc[:])
+            else:
+                nc.vector.tensor_copy(out=result[:], in_=acc[:])
+            nc.sync.dma_start(out=out[cols, :], in_=result[:])

@@ -4,6 +4,7 @@ import concourse.mybir as mybir
 
 BF16 = mybir.dt.bfloat16
 F32 = mybir.dt.float32
+I32 = mybir.dt.int32
 U32 = mybir.dt.uint32
 U8 = mybir.dt.uint8
 E4M3_X4 = mybir.dt.float8_e4m3fn_x4
@@ -16,12 +17,18 @@ BATCH = 2
 LENGTH = 256
 WIDTH = 512
 HALF = WIDTH // 2
+LOWER = 0
+UPPER = 1
 ROWS = LENGTH // P
 CHUNK = 128
 CHUNKS = WIDTH // CHUNK
 
 FLOPS = 2 * BATCH * LENGTH * WIDTH * WIDTH
 BYTES = 2 * (2 * BATCH * LENGTH * WIDTH + 2 * LENGTH * WIDTH) + 4 * WIDTH * WIDTH
+
+
+def span(first, count):
+    return slice(first, first + count)
 
 
 def tile_denseattentiononehead_pa_s_kernel(tc, hidden_states, W_q, cos, sin, grad_out, out):
@@ -32,10 +39,12 @@ def tile_denseattentiononehead_pa_s_kernel(tc, hidden_states, W_q, cos, sin, gra
     sin_rows = sin.rearrange("(p i) w -> i p w", i=ROWS)
     g_rows = grad_out.rearrange("b (p i) o -> b p i o", i=ROWS)
 
+    tokens = [b * ROWS + i for i in range(ROWS) for b in range(BATCH)]
+
     with ExitStack() as ctx:
         keep = ctx.enter_context(tc.tile_pool(name="keep", bufs=1))
-        results = ctx.enter_context(tc.tile_pool(name="results", bufs=CHUNKS))
-        psum = ctx.enter_context(tc.psum_pool(name="psum", bufs=CHUNKS))
+        results = ctx.enter_context(tc.tile_pool(name="results", bufs=2 * CHUNKS))
+        psum = ctx.enter_context(tc.psum_pool(name="psum", bufs=2 * CHUNKS))
         ctx.enter_context(tc.manual_schedule())
 
         x_sb = keep.tile([P, PACK, WIDTH], BF16)
@@ -43,98 +52,100 @@ def tile_denseattentiononehead_pa_s_kernel(tc, hidden_states, W_q, cos, sin, gra
         sin_sb = keep.tile([P, ROWS, WIDTH], BF16)
         g_sb = keep.tile([P, PACK, WIDTH], BF16)
 
-        for i in range(ROWS):
-            for b in range(BATCH):
-                nc.sync.dma_start(out=x_sb[:, b * ROWS + i, :], in_=x_rows[b, i, :, :])
-                if b == 0:
-                    nc.sync.dma_start(out=cos_sb[:, i, :], in_=cos_rows[i, :, :])
-                    nc.sync.dma_start(out=sin_sb[:, i, :], in_=sin_rows[i, :, :])
-        for b in range(BATCH):
-            nc.sync.dma_start(out=g_sb[:, b * ROWS : (b + 1) * ROWS, :], in_=g_rows[b, :, :, :])
+        h_codes = keep.tile([P, WIDTH + HALF], U32, align_bytes=64)
+        h_scales = keep.tile([P, WIDTH + HALF], U8, align_bytes=64)
+        nc.vector.memset(h_codes[:, WIDTH:].bitcast(I32), 0)
+        nc.vector.memset(h_scales[:, WIDTH:].bitcast(I32), 0)
 
-        x_cos = keep.tile([P, PACK, WIDTH], F32)
-        x_sin_hi = keep.tile([P, PACK, HALF], F32)
-        x_sin_lo = keep.tile([P, PACK, HALF], F32)
-        for i in range(ROWS):
-            for b in range(BATCH):
-                t = b * ROWS + i
-                nc.vector.tensor_tensor(
-                    out=x_cos[:, t, :], in0=x_sb[:, t, :], in1=cos_sb[:, i, :], op=ALU.mult
-                )
-                nc.vector.tensor_tensor(
-                    out=x_sin_hi[:, t, :], in0=x_sb[:, t, :HALF], in1=sin_sb[:, i, HALF:], op=ALU.mult
-                )
-                nc.vector.tensor_tensor(
-                    out=x_sin_lo[:, t, :], in0=x_sb[:, t, HALF:], in1=sin_sb[:, i, :HALF], op=ALU.mult
-                )
+        for t in tokens:
+            b, i = divmod(t, ROWS)
+            nc.sync.dma_start(out=x_sb[:, t, :], in_=x_rows[b, i, :, :])
+            if b == 0:
+                nc.sync.dma_start(out=cos_sb[:, i, :], in_=cos_rows[i, :, :])
+                nc.sync.dma_start(out=sin_sb[:, i, :], in_=sin_rows[i, :, :])
+        for b in range(BATCH):
+            nc.sync.dma_start(out=g_sb[:, span(b * ROWS, ROWS), :], in_=g_rows[b, :, :, :])
 
         g_grouped = keep.tile([P, WIDTH, PACK], BF16, align_bytes=64)
-        for c in range(CHUNKS):
-            cols = slice(c * CHUNK, (c + 1) * CHUNK)
-            nc.scalar.copy(out=g_grouped[:, cols, :], in_=g_sb[:, :, cols].rearrange("p t o -> p o t"))
-
         g_codes = keep.tile([P, WIDTH], U32, align_bytes=64)
         g_scales = keep.tile([P, WIDTH], U8, align_bytes=64)
+        for c in range(CHUNKS):
+            cols = span(c * CHUNK, CHUNK)
+            nc.scalar.copy(out=g_grouped[:, cols, :], in_=g_sb[:, :, cols].rearrange("p t o -> p o t"))
 
         def quantise_g(c):
-            cols = slice(c * CHUNK, (c + 1) * CHUNK)
+            cols = span(c * CHUNK, CHUNK)
             nc.vector.quantize_mx(
                 out=g_codes[:, cols].bitcast(E5M2_X4),
                 scales=g_scales[:, cols],
                 in_=g_grouped[:, cols, :].rearrange("p o t -> p (o t)"),
             )
 
+        x_cos = [keep.tile([P, PACK, HALF], F32, name="x_cos_%d" % half) for half in (LOWER, UPPER)]
+        x_sin = [keep.tile([P, PACK, HALF], F32, name="x_sin_%d" % half) for half in (LOWER, UPPER)]
         h_grouped = keep.tile([P, WIDTH, PACK], BF16, align_bytes=64)
-        h_codes = keep.tile([P, WIDTH], U32, align_bytes=64)
-        h_scales = keep.tile([P, WIDTH], U8, align_bytes=64)
 
-        def rotate(c):
-            cols = slice(c * CHUNK, (c + 1) * CHUNK)
-            if c * CHUNK >= HALF:
-                x_sin, op = x_sin_hi, ALU.add
-            else:
-                x_sin, op = x_sin_lo, ALU.subtract
-            half_cols = slice(c * CHUNK % HALF, c * CHUNK % HALF + CHUNK)
+        def multiply_by_cos(t, half):
             nc.vector.tensor_tensor(
-                out=h_grouped[:, cols, :],
-                in0=x_cos[:, :, cols].rearrange("p t j -> p j t"),
-                in1=x_sin[:, :, half_cols].rearrange("p t j -> p j t"),
-                op=op,
+                out=x_cos[half][:, t, :],
+                in0=x_sb[:, t, span(half * HALF, HALF)],
+                in1=cos_sb[:, t % ROWS, span(half * HALF, HALF)],
+                op=ALU.mult,
             )
 
-        def quantise_h(c):
-            cols = slice(c * CHUNK, (c + 1) * CHUNK)
-            nc.vector.quantize_mx(
-                out=h_codes[:, cols].bitcast(E4M3_X4),
-                scales=h_scales[:, cols],
-                in_=h_grouped[:, cols, :].rearrange("p j t -> p (j t)"),
+        def multiply_by_sin(t, half):
+            nc.vector.tensor_tensor(
+                out=x_sin[half][:, t, :],
+                in0=x_sb[:, t, span((1 - half) * HALF, HALF)],
+                in1=sin_sb[:, t % ROWS, span(half * HALF, HALF)],
+                op=ALU.mult,
             )
 
-        order = list(range(CHUNKS // 2, CHUNKS)) + list(range(CHUNKS // 2))
-        rotate(order[0])
-        for n in range(1, CHUNKS):
-            rotate(order[n])
-            quantise_h(order[n - 1])
-        quantise_g(0)
-        quantise_h(order[CHUNKS - 1])
-        for c in range(1, CHUNKS):
+        def finish_half_of_h(half):
+            for first in (0, CHUNK):
+                nc.vector.tensor_tensor(
+                    out=h_grouped[:, span(half * HALF + first, CHUNK), :],
+                    in0=x_cos[half][:, :, span(first, CHUNK)].rearrange("p t j -> p j t"),
+                    in1=x_sin[half][:, :, span(first, CHUNK)].rearrange("p t j -> p j t"),
+                    op=ALU.add if half == UPPER else ALU.subtract,
+                )
+            for first in (0, CHUNK):
+                cols = span(half * HALF + first, CHUNK)
+                nc.vector.quantize_mx(
+                    out=h_codes[:, cols].bitcast(E4M3_X4),
+                    scales=h_scales[:, cols],
+                    in_=h_grouped[:, cols, :].rearrange("p j t -> p (j t)"),
+                )
+
+        def multiply_half_of_h(half):
+            window = span(half * HALF, WIDTH)
+            for c in range(CHUNKS):
+                cols = span(c * CHUNK, CHUNK)
+                acc = psum.tile([CHUNK, WIDTH], F32)
+                nc.tensor.matmul_mx(
+                    out=acc[:],
+                    lhsT=g_codes[:, cols].bitcast(E5M2_X4),
+                    lhsT_scale=g_scales[:, cols],
+                    rhs=h_codes[:, window].bitcast(E4M3_X4),
+                    rhs_scale=h_scales[:, window],
+                    start=True,
+                    stop=True,
+                )
+                result = results.tile([CHUNK, HALF], F32)
+                if half == LOWER and c % 2 == 1:
+                    nc.vector.tensor_copy(out=result[:], in_=acc[:, :HALF])
+                else:
+                    nc.scalar.copy(out=result[:], in_=acc[:, :HALF])
+                nc.sync.dma_start(out=out[cols, span(half * HALF, HALF)], in_=result[:])
+
+        for t in tokens:
+            multiply_by_cos(t, UPPER)
+            multiply_by_sin(t, UPPER)
+            multiply_by_cos(t, LOWER)
+        finish_half_of_h(UPPER)
+        for c, t in enumerate(tokens):
+            multiply_by_sin(t, LOWER)
             quantise_g(c)
-
-        for c in range(CHUNKS):
-            cols = slice(c * CHUNK, (c + 1) * CHUNK)
-            acc = psum.tile([CHUNK, WIDTH], F32)
-            nc.tensor.matmul_mx(
-                out=acc[:],
-                lhsT=g_codes[:, cols].bitcast(E5M2_X4),
-                lhsT_scale=g_scales[:, cols],
-                rhs=h_codes[:].bitcast(E4M3_X4),
-                rhs_scale=h_scales[:],
-                start=True,
-                stop=True,
-            )
-            result = results.tile([CHUNK, WIDTH], F32)
-            if c % 2 == 0:
-                nc.scalar.copy(out=result[:], in_=acc[:])
-            else:
-                nc.vector.tensor_copy(out=result[:], in_=acc[:])
-            nc.sync.dma_start(out=out[cols, :], in_=result[:])
+        multiply_half_of_h(UPPER)
+        finish_half_of_h(LOWER)
+        multiply_half_of_h(LOWER)

@@ -81,16 +81,13 @@ def tile_denseattentiononehead_pa_s_kernel(tc, hidden_states, W_q, cos, sin, gra
                 in_=g_grouped[:, cols, :].rearrange("p o t -> p (o t)"),
             )
 
-        x_cos = [keep.tile([P, PACK, HALF], F32, name="x_cos_%d" % half) for half in (LOWER, UPPER)]
+        x_cos = keep.tile([P, PACK, WIDTH], F32)
         x_sin = [keep.tile([P, PACK, HALF], F32, name="x_sin_%d" % half) for half in (LOWER, UPPER)]
         h_grouped = keep.tile([P, WIDTH, PACK], BF16, align_bytes=64)
 
-        def multiply_by_cos(t, half):
+        def multiply_by_cos(t):
             nc.vector.tensor_tensor(
-                out=x_cos[half][:, t, :],
-                in0=x_sb[:, t, span(half * HALF, HALF)],
-                in1=cos_sb[:, t % ROWS, span(half * HALF, HALF)],
-                op=ALU.mult,
+                out=x_cos[:, t, :], in0=x_sb[:, t, :], in1=cos_sb[:, t % ROWS, :], op=ALU.mult
             )
 
         def multiply_by_sin(t, half):
@@ -101,21 +98,22 @@ def tile_denseattentiononehead_pa_s_kernel(tc, hidden_states, W_q, cos, sin, gra
                 op=ALU.mult,
             )
 
-        def finish_half_of_h(half):
-            for first in (0, CHUNK):
-                nc.vector.tensor_tensor(
-                    out=h_grouped[:, span(half * HALF + first, CHUNK), :],
-                    in0=x_cos[half][:, :, span(first, CHUNK)].rearrange("p t j -> p j t"),
-                    in1=x_sin[half][:, :, span(first, CHUNK)].rearrange("p t j -> p j t"),
-                    op=ALU.add if half == UPPER else ALU.subtract,
-                )
-            for first in (0, CHUNK):
-                cols = span(half * HALF + first, CHUNK)
-                nc.vector.quantize_mx(
-                    out=h_codes[:, cols].bitcast(E4M3_X4),
-                    scales=h_scales[:, cols],
-                    in_=h_grouped[:, cols, :].rearrange("p j t -> p (j t)"),
-                )
+        def add_terms(half):
+            cols = span(half * HALF, HALF)
+            nc.vector.tensor_tensor(
+                out=h_grouped[:, cols, :],
+                in0=x_cos[:, :, cols].rearrange("p t j -> p j t"),
+                in1=x_sin[half][:].rearrange("p t j -> p j t"),
+                op=ALU.add if half == UPPER else ALU.subtract,
+            )
+
+        def quantise_h(half):
+            cols = span(half * HALF, HALF)
+            nc.vector.quantize_mx(
+                out=h_codes[:, cols].bitcast(E4M3_X4),
+                scales=h_scales[:, cols],
+                in_=h_grouped[:, cols, :].rearrange("p j t -> p (j t)"),
+            )
 
         def multiply_half_of_h(half):
             window = span(half * HALF, WIDTH)
@@ -139,13 +137,18 @@ def tile_denseattentiononehead_pa_s_kernel(tc, hidden_states, W_q, cos, sin, gra
                 nc.sync.dma_start(out=out[cols, span(half * HALF, HALF)], in_=result[:])
 
         for t in tokens:
-            multiply_by_cos(t, UPPER)
+            multiply_by_cos(t)
             multiply_by_sin(t, UPPER)
-            multiply_by_cos(t, LOWER)
-        finish_half_of_h(UPPER)
-        for c, t in enumerate(tokens):
+        multiply_by_sin(tokens[0], LOWER)
+        add_terms(UPPER)
+        for t in tokens[1:]:
             multiply_by_sin(t, LOWER)
+        quantise_h(UPPER)
+        for c in range(CHUNKS - 1):
             quantise_g(c)
+        add_terms(LOWER)
+        quantise_g(CHUNKS - 1)
+        quantise_h(LOWER)
+
         multiply_half_of_h(UPPER)
-        finish_half_of_h(LOWER)
         multiply_half_of_h(LOWER)

@@ -22,6 +22,7 @@ UPPER = 1
 ROWS = LENGTH // P
 CHUNK = 128
 CHUNKS = WIDTH // CHUNK
+RUN = 2
 
 FLOPS = 2 * BATCH * LENGTH * WIDTH * WIDTH
 BYTES = 2 * (2 * BATCH * LENGTH * WIDTH + 2 * LENGTH * WIDTH) + 4 * WIDTH * WIDTH
@@ -101,9 +102,9 @@ def tile_denseattentiononehead_pa_s_kernel(tc, hidden_states, W_q, cos, sin, gra
         def add_terms(half):
             cols = span(half * HALF, HALF)
             nc.vector.tensor_tensor(
-                out=h_grouped[:, cols, :],
-                in0=x_cos[:, :, cols].rearrange("p t j -> p j t"),
-                in1=x_sin[half][:].rearrange("p t j -> p j t"),
+                out=h_grouped[:, cols, :].rearrange("p (c i) t -> p c t i", i=RUN),
+                in0=x_cos[:, :, cols].rearrange("p t (c i) -> p c t i", i=RUN),
+                in1=x_sin[half][:].rearrange("p t (c i) -> p c t i", i=RUN),
                 op=ALU.add if half == UPPER else ALU.subtract,
             )
 

@@ -1,5 +1,6 @@
 from contextlib import ExitStack
 
+import concourse.masks as masks
 import concourse.mybir as mybir
 
 BF16 = mybir.dt.bfloat16
@@ -22,6 +23,8 @@ UPPER = 1
 ROWS = LENGTH // P
 CHUNK = 128
 CHUNKS = WIDTH // CHUNK
+WARM_UP = 28
+SLOTS = 8
 RUN = 2
 
 FLOPS = 2 * BATCH * LENGTH * WIDTH * WIDTH
@@ -35,44 +38,68 @@ def span(first, count):
 def tile_denseattentiononehead_pa_s_kernel(tc, hidden_states, W_q, cos, sin, grad_out, out):
     nc = tc.nc
 
-    x_rows = hidden_states.rearrange("b (p i) w -> b i p w", i=ROWS)
+    x_rows = hidden_states.rearrange("b (p i) w -> i p b w", i=ROWS)
     cos_rows = cos.rearrange("(p i) w -> i p w", i=ROWS)
     sin_rows = sin.rearrange("(p i) w -> i p w", i=ROWS)
-    g_rows = grad_out.rearrange("b (p i) o -> b p i o", i=ROWS)
-
-    tokens = [b * ROWS + i for i in range(ROWS) for b in range(BATCH)]
+    g_rows = grad_out.rearrange("b (p i) o -> p b i o", i=ROWS)
 
     with ExitStack() as ctx:
         keep = ctx.enter_context(tc.tile_pool(name="keep", bufs=1))
         results = ctx.enter_context(tc.tile_pool(name="results", bufs=2 * CHUNKS))
-        psum = ctx.enter_context(tc.psum_pool(name="psum", bufs=2 * CHUNKS))
+        psum = ctx.enter_context(tc.psum_pool(name="psum", bufs=5))
+        tables = ctx.enter_context(tc.psum_pool(name="tables", bufs=1))
         ctx.enter_context(tc.manual_schedule())
 
-        x_sb = keep.tile([P, PACK, WIDTH], BF16)
+        x_sb = keep.tile([P, BATCH, ROWS, WIDTH], BF16)
         cos_sb = keep.tile([P, ROWS, WIDTH], BF16)
         sin_sb = keep.tile([P, ROWS, WIDTH], BF16)
-        g_sb = keep.tile([P, PACK, WIDTH], BF16)
+        g_sb = keep.tile([P, BATCH, ROWS, WIDTH], BF16)
 
         h_codes = keep.tile([P, WIDTH + HALF], U32, align_bytes=64)
         h_scales = keep.tile([P, WIDTH + HALF], U8, align_bytes=64)
         nc.vector.memset(h_codes[:, WIDTH:].bitcast(I32), 0)
         nc.vector.memset(h_scales[:, WIDTH:].bitcast(I32), 0)
 
-        for t in tokens:
-            b, i = divmod(t, ROWS)
-            nc.sync.dma_start(out=x_sb[:, t, :], in_=x_rows[b, i, :, :])
-            if b == 0:
-                nc.sync.dma_start(out=cos_sb[:, i, :], in_=cos_rows[i, :, :])
-                nc.sync.dma_start(out=sin_sb[:, i, :], in_=sin_rows[i, :, :])
-        for b in range(BATCH):
-            nc.sync.dma_start(out=g_sb[:, span(b * ROWS, ROWS), :], in_=g_rows[b, :, :, :])
+        first_in = keep.tile([P, 1], F32)
+        first_out = keep.tile([P, 1], F32)
+        nc.vector.memset(first_in[:], 0.0)
+        nc.scalar.copy(out=first_out[:], in_=first_in[:])
+
+        identity = keep.tile([P, P], BF16)
+        masks.make_identity(nc, identity[:])
+
+        steps = [(0, span(b, 1)) for b in range(BATCH)] + [(1, span(0, BATCH))]
+        def load_x(step):
+            i, batches = steps[step]
+            nc.sync.dma_start(out=x_sb[:, batches, i, :], in_=x_rows[i, :, batches, :])
+
+        def load_tables(i):
+            nc.sync.dma_start(out=cos_sb[:, i, :], in_=cos_rows[i, :, :])
+            nc.sync.dma_start(out=sin_sb[:, i, HALF:], in_=sin_rows[i, :, HALF:])
+
+        load_x(0)
+        load_tables(0)
+        load_x(1)
+        load_tables(1)
+        load_x(2)
+        nc.sync.dma_start(out=sin_sb[:, :, :HALF], in_=sin.rearrange("(p i) w -> p i w", i=ROWS)[:, :, :HALF])
+        nc.sync.dma_start(out=g_sb[:], in_=g_rows)
+
+        cos_psum = tables.tile([P, WIDTH], F32)
+        sin_psum = tables.tile([P, HALF], F32)
+        nc.tensor.matmul(out=cos_psum[:], lhsT=identity[:], rhs=cos_sb[:, 1, :], start=True, stop=True)
+        nc.tensor.matmul(out=sin_psum[:], lhsT=identity[:], rhs=sin_sb[:, 1, HALF:], start=True, stop=True)
+
+        unread = tables.tile([P, SLOTS, P], BF16)
+        for n in range(WARM_UP):
+            nc.tensor.transpose(unread[:, n % SLOTS, :], x_sb[:, 1, 1, :P], identity[:])
 
         g_grouped = keep.tile([P, WIDTH, PACK], BF16, align_bytes=64)
         g_codes = keep.tile([P, WIDTH], U32, align_bytes=64)
         g_scales = keep.tile([P, WIDTH], U8, align_bytes=64)
         for c in range(CHUNKS):
             cols = span(c * CHUNK, CHUNK)
-            nc.scalar.copy(out=g_grouped[:, cols, :], in_=g_sb[:, :, cols].rearrange("p t o -> p o t"))
+            nc.scalar.copy(out=g_grouped[:, cols, :], in_=g_sb[:, :, :, cols].rearrange("p b i o -> p o (b i)"))
 
         def quantise_g(c):
             cols = span(c * CHUNK, CHUNK)
@@ -82,34 +109,38 @@ def tile_denseattentiononehead_pa_s_kernel(tc, hidden_states, W_q, cos, sin, gra
                 in_=g_grouped[:, cols, :].rearrange("p o t -> p (o t)"),
             )
 
-        x_cos = keep.tile([P, PACK, WIDTH], F32)
-        x_sin = [keep.tile([P, PACK, HALF], F32, name="x_sin_%d" % half) for half in (LOWER, UPPER)]
+        x_cos = keep.tile([P, BATCH, ROWS, WIDTH], F32)
+        x_sin = [keep.tile([P, BATCH, ROWS, HALF], F32, name="x_sin_%d" % half) for half in (LOWER, UPPER)]
         h_grouped = keep.tile([P, WIDTH, PACK], BF16, align_bytes=64)
 
-        def multiply_by_cos(t):
-            nc.vector.tensor_tensor(
-                out=x_cos[:, t, :], in0=x_sb[:, t, :], in1=cos_sb[:, t % ROWS, :], op=ALU.mult
+        def multiply(out, x, table, engine=nc.vector):
+            engine.tensor_tensor(
+                out=out, in0=x, in1=table.unsqueeze(1).to_broadcast(x.shape), op=ALU.mult
             )
 
-        def multiply_by_sin(t, half):
-            nc.vector.tensor_tensor(
-                out=x_sin[half][:, t, :],
-                in0=x_sb[:, t, span((1 - half) * HALF, HALF)],
-                in1=sin_sb[:, t % ROWS, span(half * HALF, HALF)],
-                op=ALU.mult,
+        def multiply_by_cos(i, batches):
+            table = cos_psum[:] if i == 1 else cos_sb[:, i, :]
+            multiply(x_cos[:, batches, i, :], x_sb[:, batches, i, :], table)
+
+        def multiply_by_sin(i, batches, half, engine=nc.vector):
+            table = sin_psum[:] if i == 1 and half == UPPER else sin_sb[:, i, span(half * HALF, HALF)]
+            multiply(
+                x_sin[half][:, batches, i, :],
+                x_sb[:, batches, i, span((1 - half) * HALF, HALF)],
+                table,
+                engine,
             )
 
-        def add_terms(half):
-            cols = span(half * HALF, HALF)
+        def add_terms(half, cols):
+            within = slice(cols.start - half * HALF, cols.stop - half * HALF)
             nc.vector.tensor_tensor(
-                out=h_grouped[:, cols, :].rearrange("p (c i) t -> p c t i", i=RUN),
-                in0=x_cos[:, :, cols].rearrange("p t (c i) -> p c t i", i=RUN),
-                in1=x_sin[half][:].rearrange("p t (c i) -> p c t i", i=RUN),
+                out=h_grouped[:, cols, :].rearrange("p (c r) t -> p c t r", r=RUN),
+                in0=x_cos[:, :, :, cols].rearrange("p b i (c r) -> p c (b i) r", r=RUN),
+                in1=x_sin[half][:, :, :, within].rearrange("p b i (c r) -> p c (b i) r", r=RUN),
                 op=ALU.add if half == UPPER else ALU.subtract,
             )
 
-        def quantise_h(half):
-            cols = span(half * HALF, HALF)
+        def quantise_h(cols):
             nc.vector.quantize_mx(
                 out=h_codes[:, cols].bitcast(E4M3_X4),
                 scales=h_scales[:, cols],
@@ -137,19 +168,21 @@ def tile_denseattentiononehead_pa_s_kernel(tc, hidden_states, W_q, cos, sin, gra
                     nc.scalar.copy(out=result[:], in_=acc[:, :HALF])
                 nc.sync.dma_start(out=out[cols, span(half * HALF, HALF)], in_=result[:])
 
-        for t in tokens:
-            multiply_by_cos(t)
-            multiply_by_sin(t, UPPER)
-        multiply_by_sin(tokens[0], LOWER)
-        add_terms(UPPER)
-        for t in tokens[1:]:
-            multiply_by_sin(t, LOWER)
-        quantise_h(UPPER)
-        for c in range(CHUNKS - 1):
+        for i, batches in steps:
+            multiply_by_cos(i, batches)
+            multiply_by_sin(i, batches, UPPER)
+        multiply_by_sin(0, span(0, BATCH), LOWER, nc.gpsimd)
+        multiply_by_sin(1, span(0, 1), LOWER)
+        add_terms(UPPER, span(HALF, HALF))
+        multiply_by_sin(1, span(1, 1), LOWER)
+        quantise_h(span(HALF, HALF))
+        for c in range(CHUNKS):
             quantise_g(c)
-        add_terms(LOWER)
-        quantise_g(CHUNKS - 1)
-        quantise_h(LOWER)
+        quarters = [span(q * HALF // 2, HALF // 2) for q in range(2)]
+        for cols in quarters:
+            add_terms(LOWER, cols)
+        for cols in quarters:
+            quantise_h(cols)
 
         multiply_half_of_h(UPPER)
         multiply_half_of_h(LOWER)

@@ -45,7 +45,7 @@ def tile_denseattentiononehead_pa_s_kernel(tc, hidden_states, W_q, cos, sin, gra
 
     with ExitStack() as ctx:
         keep = ctx.enter_context(tc.tile_pool(name="keep", bufs=1))
-        results = ctx.enter_context(tc.tile_pool(name="results", bufs=2 * CHUNKS))
+        results = ctx.enter_context(tc.tile_pool(name="results", bufs=10))
         psum = ctx.enter_context(tc.psum_pool(name="psum", bufs=5))
         tables = ctx.enter_context(tc.psum_pool(name="tables", bufs=1))
         ctx.enter_context(tc.manual_schedule())
@@ -101,8 +101,7 @@ def tile_denseattentiononehead_pa_s_kernel(tc, hidden_states, W_q, cos, sin, gra
             cols = span(c * CHUNK, CHUNK)
             nc.scalar.copy(out=g_grouped[:, cols, :], in_=g_sb[:, :, :, cols].rearrange("p b i o -> p o (b i)"))
 
-        def quantise_g(c):
-            cols = span(c * CHUNK, CHUNK)
+        def quantise_g(cols):
             nc.vector.quantize_mx(
                 out=g_codes[:, cols].bitcast(E5M2_X4),
                 scales=g_scales[:, cols],
@@ -147,9 +146,10 @@ def tile_denseattentiononehead_pa_s_kernel(tc, hidden_states, W_q, cos, sin, gra
                 in_=h_grouped[:, cols, :].rearrange("p j t -> p (j t)"),
             )
 
-        def multiply_half_of_h(half):
-            window = span(half * HALF, WIDTH)
-            for c in range(CHUNKS):
+        def finish(chunks, js):
+            window = span(js.start, WIDTH)
+            width = js.stop - js.start
+            for c, copy in chunks:
                 cols = span(c * CHUNK, CHUNK)
                 acc = psum.tile([CHUNK, WIDTH], F32)
                 nc.tensor.matmul_mx(
@@ -161,28 +161,30 @@ def tile_denseattentiononehead_pa_s_kernel(tc, hidden_states, W_q, cos, sin, gra
                     start=True,
                     stop=True,
                 )
-                result = results.tile([CHUNK, HALF], F32)
-                if half == LOWER and c % 2 == 1:
-                    nc.vector.tensor_copy(out=result[:], in_=acc[:, :HALF])
-                else:
-                    nc.scalar.copy(out=result[:], in_=acc[:, :HALF])
-                nc.sync.dma_start(out=out[cols, span(half * HALF, HALF)], in_=result[:])
+                result = results.tile([CHUNK, width], F32)
+                copy(out=result[:], in_=acc[:, :width])
+                nc.sync.dma_start(out=out[cols, js], in_=result[:])
 
         for i, batches in steps:
             multiply_by_cos(i, batches)
             multiply_by_sin(i, batches, UPPER)
         multiply_by_sin(0, span(0, BATCH), LOWER, nc.gpsimd)
-        multiply_by_sin(1, span(0, 1), LOWER)
+        multiply_by_sin(1, span(0, BATCH), LOWER)
         add_terms(UPPER, span(HALF, HALF))
-        multiply_by_sin(1, span(1, 1), LOWER)
+        quantise_g(span(0, HALF))
         quantise_h(span(HALF, HALF))
-        for c in range(CHUNKS):
-            quantise_g(c)
-        quarters = [span(q * HALF // 2, HALF // 2) for q in range(2)]
-        for cols in quarters:
-            add_terms(LOWER, cols)
-        for cols in quarters:
-            quantise_h(cols)
+        quantise_g(span(HALF, HALF))
+        second = span(HALF // 2, HALF // 2)
+        third = [span(q * HALF // 4, HALF // 4) for q in range(2)]
+        add_terms(LOWER, second)
+        add_terms(LOWER, third[0])
+        quantise_h(second)
+        add_terms(LOWER, third[1])
+        quantise_h(third[0])
+        quantise_h(third[1])
 
-        multiply_half_of_h(UPPER)
-        multiply_half_of_h(LOWER)
+        vector, scalar = nc.vector.tensor_copy, nc.scalar.copy
+        finish([(c, scalar) for c in range(CHUNKS)], span(HALF, HALF))
+        finish([(0, scalar), (1, scalar)], second)
+        finish([(2, vector), (3, scalar)], span(0, HALF))
+        finish([(0, vector), (1, scalar)], span(0, HALF // 2))

@@ -23,6 +23,7 @@ UPPER = 1
 ROWS = LENGTH // P
 CHUNK = 128
 CHUNKS = WIDTH // CHUNK
+G_RUN = 4
 WARM_UP = 28
 SLOTS = 8
 RUN = 2
@@ -99,7 +100,10 @@ def tile_denseattentiononehead_pa_s_kernel(tc, hidden_states, W_q, cos, sin, gra
         g_scales = keep.tile([P, WIDTH], U8, align_bytes=64)
         for c in range(CHUNKS):
             cols = span(c * CHUNK, CHUNK)
-            nc.scalar.copy(out=g_grouped[:, cols, :], in_=g_sb[:, :, :, cols].rearrange("p b i o -> p o (b i)"))
+            nc.scalar.copy(
+                out=g_grouped[:, cols, :].rearrange("p (c r) t -> p c t r", r=G_RUN),
+                in_=g_sb[:, :, :, cols].rearrange("p b i (c r) -> p c (b i) r", r=G_RUN),
+            )
 
         def quantise_g(cols):
             nc.vector.quantize_mx(

@@ -24,8 +24,6 @@ ROWS = LENGTH // P
 CHUNK = 128
 CHUNKS = WIDTH // CHUNK
 G_RUN = 4
-WARM_UP = 28
-SLOTS = 8
 RUN = 2
 
 FLOPS = 2 * BATCH * LENGTH * WIDTH * WIDTH
@@ -56,8 +54,8 @@ def tile_denseattentiononehead_pa_s_kernel(tc, hidden_states, W_q, cos, sin, gra
         sin_sb = keep.tile([P, ROWS, WIDTH], BF16)
         g_sb = keep.tile([P, BATCH, ROWS, WIDTH], BF16)
 
-        h_codes = keep.tile([P, WIDTH + HALF], U32, align_bytes=64)
-        h_scales = keep.tile([P, WIDTH + HALF], U8, align_bytes=64)
+        h_codes = keep.tile([P, 2 * WIDTH], U32, align_bytes=64)
+        h_scales = keep.tile([P, 2 * WIDTH], U8, align_bytes=64)
         nc.vector.memset(h_codes[:, WIDTH:].bitcast(I32), 0)
         nc.vector.memset(h_scales[:, WIDTH:].bitcast(I32), 0)
 
@@ -74,30 +72,29 @@ def tile_denseattentiononehead_pa_s_kernel(tc, hidden_states, W_q, cos, sin, gra
             i, batches = steps[step]
             nc.sync.dma_start(out=x_sb[:, batches, i, :], in_=x_rows[i, :, batches, :])
 
-        def load_tables(i):
+        def load_cos(i):
             nc.sync.dma_start(out=cos_sb[:, i, :], in_=cos_rows[i, :, :])
-            nc.sync.dma_start(out=sin_sb[:, i, HALF:], in_=sin_rows[i, :, HALF:])
+
+        def load_sin(i):
+            nc.sync.dma_start(out=sin_sb[:, i, :], in_=sin_rows[i, :, :])
 
         load_x(0)
-        load_tables(0)
+        load_cos(0)
+        load_sin(0)
         load_x(1)
-        load_tables(1)
+        load_cos(1)
         load_x(2)
-        nc.sync.dma_start(out=sin_sb[:, :, :HALF], in_=sin.rearrange("(p i) w -> p i w", i=ROWS)[:, :, :HALF])
+        load_sin(1)
         nc.sync.dma_start(out=g_sb[:], in_=g_rows)
 
         cos_psum = tables.tile([P, WIDTH], F32)
         sin_psum = tables.tile([P, HALF], F32)
-        nc.tensor.matmul(out=cos_psum[:], lhsT=identity[:], rhs=cos_sb[:, 1, :], start=True, stop=True)
-        nc.tensor.matmul(out=sin_psum[:], lhsT=identity[:], rhs=sin_sb[:, 1, HALF:], start=True, stop=True)
-
-        unread = tables.tile([P, SLOTS, P], BF16)
-        for n in range(WARM_UP):
-            nc.tensor.transpose(unread[:, n % SLOTS, :], x_sb[:, 1, 1, :P], identity[:])
 
         g_grouped = keep.tile([P, WIDTH, PACK], BF16, align_bytes=64)
-        g_codes = keep.tile([P, WIDTH], U32, align_bytes=64)
-        g_scales = keep.tile([P, WIDTH], U8, align_bytes=64)
+        g_codes = keep.tile([P, WIDTH + CHUNK], U32, align_bytes=64)
+        g_scales = keep.tile([P, WIDTH + CHUNK], U8, align_bytes=64)
+        nc.vector.memset(g_codes[:, WIDTH:].bitcast(I32), 0)
+        nc.vector.memset(g_scales[:, WIDTH:].bitcast(I32), 0)
         for c in range(CHUNKS):
             cols = span(c * CHUNK, CHUNK)
             nc.scalar.copy(
@@ -153,7 +150,7 @@ def tile_denseattentiononehead_pa_s_kernel(tc, hidden_states, W_q, cos, sin, gra
         def finish(chunks, js):
             window = span(js.start, WIDTH)
             width = js.stop - js.start
-            for c, copy in chunks:
+            for c, copy, queue in chunks:
                 cols = span(c * CHUNK, CHUNK)
                 acc = psum.tile([CHUNK, WIDTH], F32)
                 nc.tensor.matmul_mx(
@@ -167,13 +164,39 @@ def tile_denseattentiononehead_pa_s_kernel(tc, hidden_states, W_q, cos, sin, gra
                 )
                 result = results.tile([CHUNK, width], F32)
                 copy(out=result[:], in_=acc[:, :width])
-                nc.sync.dma_start(out=out[cols, js], in_=result[:])
+                queue.dma_start(out=out[cols, js], in_=result[:])
 
-        for i, batches in steps:
-            multiply_by_cos(i, batches)
-            multiply_by_sin(i, batches, UPPER)
-        multiply_by_sin(0, span(0, BATCH), LOWER, nc.gpsimd)
-        multiply_by_sin(1, span(0, BATCH), LOWER)
+        def warm_up(lhs, count):
+            acc = psum.tile([CHUNK, WIDTH], F32)
+            for n in range(count):
+                nc.tensor.matmul_mx(
+                    out=acc[:],
+                    lhsT=g_codes[:, lhs].bitcast(E5M2_X4),
+                    lhsT_scale=g_scales[:, lhs],
+                    rhs=h_codes[:, WIDTH:].bitcast(E4M3_X4),
+                    rhs_scale=h_scales[:, WIDTH:],
+                    start=n == 0,
+                    stop=n == count - 1,
+                )
+
+        warm_up(span(WIDTH, CHUNK), 3)
+
+        nc.tensor.matmul(out=cos_psum[:], lhsT=identity[:], rhs=cos_sb[:, 1, :], start=True, stop=True)
+        nc.tensor.matmul(out=sin_psum[:], lhsT=identity[:], rhs=sin_sb[:, 1, HALF:], start=True, stop=True)
+
+        warm_up(span(WIDTH, CHUNK), 9)
+
+        both = span(0, BATCH)
+        first, last = span(0, 1), span(1, 1)
+        multiply_by_cos(0, first)
+        multiply_by_sin(0, first, UPPER)
+        multiply_by_sin(0, first, LOWER)
+        multiply_by_cos(0, last)
+        multiply_by_sin(0, last, UPPER)
+        multiply_by_cos(1, both)
+        multiply_by_sin(1, both, UPPER)
+        multiply_by_sin(1, both, LOWER, nc.gpsimd)
+        multiply_by_sin(0, last, LOWER)
         add_terms(UPPER, span(HALF, HALF))
         quantise_g(span(0, HALF))
         quantise_h(span(HALF, HALF))
@@ -188,7 +211,7 @@ def tile_denseattentiononehead_pa_s_kernel(tc, hidden_states, W_q, cos, sin, gra
         quantise_h(third[1])
 
         vector, scalar = nc.vector.tensor_copy, nc.scalar.copy
-        finish([(c, scalar) for c in range(CHUNKS)], span(HALF, HALF))
-        finish([(0, scalar), (1, scalar)], second)
-        finish([(2, vector), (3, scalar)], span(0, HALF))
-        finish([(0, vector), (1, scalar)], span(0, HALF // 2))
+        finish([(c, scalar, nc.sync) for c in range(CHUNKS)], span(HALF, HALF))
+        finish([(0, scalar, nc.sync), (1, scalar, nc.sync)], second)
+        finish([(2, vector, nc.sync), (3, scalar, nc.sync)], span(0, HALF))
+        finish([(0, vector, nc.sync), (1, scalar, nc.scalar)], span(0, HALF // 2))

@@ -24,7 +24,7 @@ ROWS = LENGTH // P
 CHUNK = 128
 CHUNKS = WIDTH // CHUNK
 G_RUN = 4
-RUN = 2
+RUN = 4
 
 FLOPS = 2 * BATCH * LENGTH * WIDTH * WIDTH
 BYTES = 2 * (2 * BATCH * LENGTH * WIDTH + 2 * LENGTH * WIDTH) + 4 * WIDTH * WIDTH

@@ -67,22 +67,25 @@ def tile_denseattentiononehead_pa_s_kernel(tc, hidden_states, W_q, cos, sin, gra
         identity = keep.tile([P, P], BF16)
         masks.make_identity(nc, identity[:])
 
+        both, first, last = span(0, BATCH), span(0, 1), span(1, 1)
+        every, upper, lower = span(0, WIDTH), span(HALF, HALF), span(0, HALF)
         steps = [(0, span(b, 1)) for b in range(BATCH)] + [(1, span(0, BATCH))]
         def load_x(step):
             i, batches = steps[step]
             nc.sync.dma_start(out=x_sb[:, batches, i, :], in_=x_rows[i, :, batches, :])
 
-        def load_cos(i):
-            nc.sync.dma_start(out=cos_sb[:, i, :], in_=cos_rows[i, :, :])
+        def load_cos(i, cols):
+            nc.sync.dma_start(out=cos_sb[:, i, cols], in_=cos_rows[i, :, cols])
 
         def load_sin(i):
             nc.sync.dma_start(out=sin_sb[:, i, :], in_=sin_rows[i, :, :])
 
         load_x(0)
-        load_cos(0)
+        load_cos(0, upper)
+        load_cos(0, lower)
         load_sin(0)
         load_x(1)
-        load_cos(1)
+        load_cos(1, every)
         load_x(2)
         load_sin(1)
         nc.sync.dma_start(out=g_sb[:], in_=g_rows)
@@ -110,7 +113,7 @@ def tile_denseattentiononehead_pa_s_kernel(tc, hidden_states, W_q, cos, sin, gra
             )
 
         x_cos = keep.tile([P, BATCH, ROWS, WIDTH], F32)
-        x_sin = [keep.tile([P, BATCH, ROWS, HALF], F32, name="x_sin_%d" % half) for half in (LOWER, UPPER)]
+        x_sin = keep.tile([P, BATCH, ROWS, WIDTH], F32)
         h_grouped = keep.tile([P, WIDTH, PACK], BF16, align_bytes=64)
 
         def multiply(out, x, table, engine=nc.vector):
@@ -118,25 +121,32 @@ def tile_denseattentiononehead_pa_s_kernel(tc, hidden_states, W_q, cos, sin, gra
                 out=out, in0=x, in1=table.unsqueeze(1).to_broadcast(x.shape), op=ALU.mult
             )
 
-        def multiply_by_cos(i, batches):
-            table = cos_psum[:] if i == 1 else cos_sb[:, i, :]
-            multiply(x_cos[:, batches, i, :], x_sb[:, batches, i, :], table)
+        def multiply_by_cos(i, batches, cols):
+            table = cos_psum[:, cols] if i == 1 else cos_sb[:, i, cols]
+            multiply(x_cos[:, batches, i, cols], x_sb[:, batches, i, cols], table)
 
         def multiply_by_sin(i, batches, half, engine=nc.vector):
             table = sin_psum[:] if i == 1 and half == UPPER else sin_sb[:, i, span(half * HALF, HALF)]
             multiply(
-                x_sin[half][:, batches, i, :],
+                x_sin[:, batches, i, span(half * HALF, HALF)],
                 x_sb[:, batches, i, span((1 - half) * HALF, HALF)],
                 table,
                 engine,
             )
 
+        def multiply_token_by_sin(b, i):
+            nc.vector.tensor_tensor(
+                out=x_sin[:, b, i, :].rearrange("p (h w) -> p h w", w=HALF),
+                in0=x_sb[:, b, i, :].rearrange("p (h w) -> p h w", w=HALF)[:, ::-1, :],
+                in1=sin_sb[:, i, :].rearrange("p (h w) -> p h w", w=HALF),
+                op=ALU.mult,
+            )
+
         def add_terms(half, cols):
-            within = slice(cols.start - half * HALF, cols.stop - half * HALF)
             nc.vector.tensor_tensor(
                 out=h_grouped[:, cols, :].rearrange("p (c r) t -> p c t r", r=RUN),
                 in0=x_cos[:, :, :, cols].rearrange("p b i (c r) -> p c (b i) r", r=RUN),
-                in1=x_sin[half][:, :, :, within].rearrange("p b i (c r) -> p c (b i) r", r=RUN),
+                in1=x_sin[:, :, :, cols].rearrange("p b i (c r) -> p c (b i) r", r=RUN),
                 op=ALU.add if half == UPPER else ALU.subtract,
             )
 
@@ -186,32 +196,27 @@ def tile_denseattentiononehead_pa_s_kernel(tc, hidden_states, W_q, cos, sin, gra
 
         warm_up(span(WIDTH, CHUNK), 9)
 
-        both = span(0, BATCH)
-        first, last = span(0, 1), span(1, 1)
-        multiply_by_cos(0, first)
-        multiply_by_sin(0, first, UPPER)
-        multiply_by_sin(0, first, LOWER)
-        multiply_by_cos(0, last)
-        multiply_by_sin(0, last, UPPER)
-        multiply_by_cos(1, both)
+        multiply_by_cos(0, first, upper)
+        multiply_by_cos(0, first, lower)
+        multiply_token_by_sin(0, 0)
+        multiply_by_cos(0, last, every)
+        multiply_token_by_sin(1, 0)
+        multiply_by_cos(1, both, upper)
         multiply_by_sin(1, both, UPPER)
+        multiply_by_cos(1, both, lower)
         multiply_by_sin(1, both, LOWER, nc.gpsimd)
-        multiply_by_sin(0, last, LOWER)
         add_terms(UPPER, span(HALF, HALF))
         quantise_g(span(0, HALF))
         quantise_h(span(HALF, HALF))
         quantise_g(span(HALF, HALF))
-        second = span(HALF // 2, HALF // 2)
-        third = [span(q * HALF // 4, HALF // 4) for q in range(2)]
-        add_terms(LOWER, second)
-        add_terms(LOWER, third[0])
-        quantise_h(second)
-        add_terms(LOWER, third[1])
-        quantise_h(third[0])
-        quantise_h(third[1])
+        quarters = [span(q * HALF // 2, HALF // 2) for q in (1, 0)]
+        for cols in quarters:
+            add_terms(LOWER, cols)
+        for cols in quarters:
+            quantise_h(cols)
 
         vector, scalar = nc.vector.tensor_copy, nc.scalar.copy
         finish([(c, scalar, nc.sync) for c in range(CHUNKS)], span(HALF, HALF))
-        finish([(0, scalar, nc.sync), (1, scalar, nc.sync)], second)
-        finish([(2, vector, nc.sync), (3, scalar, nc.sync)], span(0, HALF))
-        finish([(0, vector, nc.sync), (1, scalar, nc.scalar)], span(0, HALF // 2))
+        finish([(0, scalar, nc.sync)], quarters[0])
+        finish([(1, vector, nc.sync), (2, scalar, nc.sync), (3, vector, nc.sync)], lower)
+        finish([(0, scalar, nc.scalar)], quarters[1])

@@ -208,10 +208,10 @@ def tile_denseattentiononehead_pa_s_kernel(tc, hidden_states, W_q, cos, sin, gra
         add_terms(UPPER, span(HALF, HALF))
         quantise_g(span(0, HALF))
         quantise_h(span(HALF, HALF))
-        quantise_g(span(HALF, HALF))
         quarters = [span(q * HALF // 2, HALF // 2) for q in (1, 0)]
-        for cols in quarters:
-            add_terms(LOWER, cols)
+        add_terms(LOWER, quarters[0])
+        quantise_g(span(HALF, HALF))
+        add_terms(LOWER, quarters[1])
         for cols in quarters:
             quantise_h(cols)
 

@@ -40,7 +40,7 @@ def tile_denseattentiononehead_pa_s_kernel(tc, hidden_states, W_q, cos, sin, gra
     x_rows = hidden_states.rearrange("b (p i) w -> i p b w", i=ROWS)
     cos_rows = cos.rearrange("(p i) w -> i p w", i=ROWS)
     sin_rows = sin.rearrange("(p i) w -> i p w", i=ROWS)
-    g_rows = grad_out.rearrange("b (p i) o -> p b i o", i=ROWS)
+    g_rows = grad_out.rearrange("b (p i) o -> b p i o", i=ROWS)
 
     with ExitStack() as ctx:
         keep = ctx.enter_context(tc.tile_pool(name="keep", bufs=1))
@@ -88,7 +88,9 @@ def tile_denseattentiononehead_pa_s_kernel(tc, hidden_states, W_q, cos, sin, gra
         load_cos(1, every)
         load_x(2)
         load_sin(1)
-        nc.sync.dma_start(out=g_sb[:], in_=g_rows)
+        for half in (lower, upper):
+            for b in range(BATCH):
+                nc.sync.dma_start(out=g_sb[:, b, :, half], in_=g_rows[b, :, :, half])
 
         cos_psum = tables.tile([P, WIDTH], F32)
         sin_psum = tables.tile([P, HALF], F32)

@@ -83,11 +83,11 @@ def tile_denseattentiononehead_pa_s_kernel(tc, hidden_states, W_q, cos, sin, gra
         load_x(0)
         load_cos(0, upper)
         load_cos(0, lower)
-        load_sin(0)
         load_x(1)
+        load_sin(0)
         load_cos(1, every)
-        load_x(2)
         load_sin(1)
+        load_x(2)
         for half in (lower, upper):
             for b in range(BATCH):
                 nc.sync.dma_start(out=g_sb[:, b, :, half], in_=g_rows[b, :, :, half])
@@ -136,13 +136,10 @@ def tile_denseattentiononehead_pa_s_kernel(tc, hidden_states, W_q, cos, sin, gra
                 engine,
             )
 
-        def multiply_token_by_sin(b, i):
-            nc.vector.tensor_tensor(
-                out=x_sin[:, b, i, :].rearrange("p (h w) -> p h w", w=HALF),
-                in0=x_sb[:, b, i, :].rearrange("p (h w) -> p h w", w=HALF)[:, ::-1, :],
-                in1=sin_sb[:, i, :].rearrange("p (h w) -> p h w", w=HALF),
-                op=ALU.mult,
-            )
+        def multiply_both_halves_by_sin(i):
+            x = x_sb[:, :, i, :].rearrange("p b (h w) -> p b h w", w=HALF)[:, :, ::-1, :]
+            table = sin_sb[:, i, :].rearrange("p (h w) -> p h w", w=HALF)
+            multiply(x_sin[:, :, i, :].rearrange("p b (h w) -> p b h w", w=HALF), x, table)
 
         def add_terms(half, cols):
             nc.vector.tensor_tensor(
@@ -196,13 +193,13 @@ def tile_denseattentiononehead_pa_s_kernel(tc, hidden_states, W_q, cos, sin, gra
         nc.tensor.matmul(out=cos_psum[:], lhsT=identity[:], rhs=cos_sb[:, 1, :], start=True, stop=True)
         nc.tensor.matmul(out=sin_psum[:], lhsT=identity[:], rhs=sin_sb[:, 1, HALF:], start=True, stop=True)
 
-        warm_up(span(WIDTH, CHUNK), 9)
+        warm_up(span(WIDTH, CHUNK), 11)
 
         multiply_by_cos(0, first, upper)
         multiply_by_cos(0, first, lower)
-        multiply_token_by_sin(0, 0)
         multiply_by_cos(0, last, every)
-        multiply_token_by_sin(1, 0)
+        multiply_both_halves_by_sin(0)
+        nc.vector.memset(x_sin[:, 1, 1, 0:1], 0.0)
         multiply_by_cos(1, both, upper)
         multiply_by_sin(1, both, UPPER)
         multiply_by_cos(1, both, lower)

@@ -175,8 +175,7 @@ def tile_denseattentiononehead_pa_s_kernel(tc, hidden_states, W_q, cos, sin, gra
                 copy(out=result[:], in_=acc[:, :width])
                 queue.dma_start(out=out[cols, js], in_=result[:])
 
-        def warm_up(lhs, count):
-            acc = psum.tile([CHUNK, WIDTH], F32)
+        def warm_up(acc, count, lhs=span(WIDTH, CHUNK)):
             for n in range(count):
                 nc.tensor.matmul_mx(
                     out=acc[:],
@@ -188,12 +187,13 @@ def tile_denseattentiononehead_pa_s_kernel(tc, hidden_states, W_q, cos, sin, gra
                     stop=n == count - 1,
                 )
 
-        warm_up(span(WIDTH, CHUNK), 3)
+        unread = psum.tile([CHUNK, WIDTH], F32, name="acc")
+        warm_up(unread, 3)
 
         nc.tensor.matmul(out=cos_psum[:], lhsT=identity[:], rhs=cos_sb[:, 1, :], start=True, stop=True)
         nc.tensor.matmul(out=sin_psum[:], lhsT=identity[:], rhs=sin_sb[:, 1, HALF:], start=True, stop=True)
 
-        warm_up(span(WIDTH, CHUNK), 11)
+        warm_up(unread, 5)
 
         multiply_by_cos(0, first, upper)
         multiply_by_cos(0, first, lower)
@@ -204,8 +204,10 @@ def tile_denseattentiononehead_pa_s_kernel(tc, hidden_states, W_q, cos, sin, gra
         multiply_by_sin(1, both, UPPER)
         multiply_by_cos(1, both, lower)
         multiply_by_sin(1, both, LOWER, nc.gpsimd)
+        warm_up(cos_psum, 4)
         add_terms(UPPER, span(HALF, HALF))
         quantise_g(span(0, HALF))
+        warm_up(cos_psum, 1, span(0, CHUNK))
         quantise_h(span(HALF, HALF))
         quarters = [span(q * HALF // 2, HALF // 2) for q in (1, 0)]
         add_terms(LOWER, quarters[0])
@@ -215,7 +217,9 @@ def tile_denseattentiononehead_pa_s_kernel(tc, hidden_states, W_q, cos, sin, gra
             quantise_h(cols)
 
         vector, scalar = nc.vector.tensor_copy, nc.scalar.copy
-        finish([(c, scalar, nc.sync) for c in range(CHUNKS)], span(HALF, HALF))
+        for chunks in ((0, 1), (2, 3)):
+            finish([(c, scalar, nc.sync) for c in chunks], span(HALF, HALF))
+            warm_up(cos_psum, 1)
         finish([(0, scalar, nc.sync)], quarters[0])
         finish([(1, vector, nc.sync), (2, scalar, nc.sync), (3, vector, nc.sync)], lower)
         finish([(0, scalar, nc.scalar)], quarters[1])

@@ -39,7 +39,7 @@ def tile_denseattentiononehead_pa_s_kernel(tc, hidden_states, W_q, cos, sin, gra
 
     x_rows = hidden_states.rearrange("b (p i) w -> i p b w", i=ROWS)
     cos_rows = cos.rearrange("(p i) w -> i p w", i=ROWS)
-    sin_rows = sin.rearrange("(p i) w -> i p w", i=ROWS)
+    sin_rows = sin.rearrange("(p i) w -> p i w", i=ROWS)
     g_rows = grad_out.rearrange("b (p i) o -> b p i o", i=ROWS)
 
     with ExitStack() as ctx:
@@ -69,28 +69,29 @@ def tile_denseattentiononehead_pa_s_kernel(tc, hidden_states, W_q, cos, sin, gra
 
         both, first, last = span(0, BATCH), span(0, 1), span(1, 1)
         every, upper, lower = span(0, WIDTH), span(HALF, HALF), span(0, HALF)
-        steps = [(0, span(b, 1)) for b in range(BATCH)] + [(1, span(0, BATCH))]
-        def load_x(step):
-            i, batches = steps[step]
-            nc.sync.dma_start(out=x_sb[:, batches, i, :], in_=x_rows[i, :, batches, :])
+
+        def load_x(i, b):
+            nc.sync.dma_start(out=x_sb[:, b, i, :], in_=x_rows[i, :, b, :])
 
         def load_cos(i, cols):
             nc.sync.dma_start(out=cos_sb[:, i, cols], in_=cos_rows[i, :, cols])
 
-        def load_sin(i):
-            nc.sync.dma_start(out=sin_sb[:, i, :], in_=sin_rows[i, :, :])
+        def load_g(b, cols):
+            nc.sync.dma_start(out=g_sb[:, b, :, cols], in_=g_rows[b, :, :, cols])
 
-        load_x(0)
+        load_x(0, 0)
         load_cos(0, upper)
         load_cos(0, lower)
-        load_x(1)
-        load_sin(0)
+        load_x(0, 1)
+        nc.sync.dma_start(out=sin_sb[:], in_=sin_rows)
         load_cos(1, every)
-        load_sin(1)
-        load_x(2)
-        for half in (lower, upper):
+        load_x(1, 0)
+        load_g(0, span(0, CHUNK))
+        load_x(1, 1)
+        load_g(1, span(0, CHUNK))
+        for cols in (span(CHUNK, CHUNK), upper):
             for b in range(BATCH):
-                nc.sync.dma_start(out=g_sb[:, b, :, half], in_=g_rows[b, :, :, half])
+                load_g(b, cols)
 
         cos_psum = tables.tile([P, WIDTH], F32)
         sin_psum = tables.tile([P, HALF], F32)
@@ -175,39 +176,37 @@ def tile_denseattentiononehead_pa_s_kernel(tc, hidden_states, W_q, cos, sin, gra
                 copy(out=result[:], in_=acc[:, :width])
                 queue.dma_start(out=out[cols, js], in_=result[:])
 
-        def warm_up(acc, count, lhs=span(WIDTH, CHUNK)):
+        def warm_up(count):
+            acc = psum.tile([CHUNK, WIDTH], F32)
             for n in range(count):
                 nc.tensor.matmul_mx(
                     out=acc[:],
-                    lhsT=g_codes[:, lhs].bitcast(E5M2_X4),
-                    lhsT_scale=g_scales[:, lhs],
+                    lhsT=g_codes[:, WIDTH:].bitcast(E5M2_X4),
+                    lhsT_scale=g_scales[:, WIDTH:],
                     rhs=h_codes[:, WIDTH:].bitcast(E4M3_X4),
                     rhs_scale=h_scales[:, WIDTH:],
                     start=n == 0,
                     stop=n == count - 1,
                 )
 
-        unread = psum.tile([CHUNK, WIDTH], F32, name="acc")
-        warm_up(unread, 3)
+        warm_up(3)
 
         nc.tensor.matmul(out=cos_psum[:], lhsT=identity[:], rhs=cos_sb[:, 1, :], start=True, stop=True)
         nc.tensor.matmul(out=sin_psum[:], lhsT=identity[:], rhs=sin_sb[:, 1, HALF:], start=True, stop=True)
 
-        warm_up(unread, 5)
+        warm_up(10)
 
         multiply_by_cos(0, first, upper)
         multiply_by_cos(0, first, lower)
         multiply_by_cos(0, last, every)
         multiply_both_halves_by_sin(0)
-        nc.vector.memset(x_sin[:, 1, 1, 0:1], 0.0)
-        multiply_by_cos(1, both, upper)
+        multiply_by_cos(1, first, every)
+        multiply_by_cos(1, last, upper)
         multiply_by_sin(1, both, UPPER)
-        multiply_by_cos(1, both, lower)
+        multiply_by_cos(1, last, lower)
         multiply_by_sin(1, both, LOWER, nc.gpsimd)
-        warm_up(cos_psum, 4)
         add_terms(UPPER, span(HALF, HALF))
         quantise_g(span(0, HALF))
-        warm_up(cos_psum, 1, span(0, CHUNK))
         quantise_h(span(HALF, HALF))
         quarters = [span(q * HALF // 2, HALF // 2) for q in (1, 0)]
         add_terms(LOWER, quarters[0])
@@ -217,9 +216,7 @@ def tile_denseattentiononehead_pa_s_kernel(tc, hidden_states, W_q, cos, sin, gra
             quantise_h(cols)
 
         vector, scalar = nc.vector.tensor_copy, nc.scalar.copy
-        for chunks in ((0, 1), (2, 3)):
-            finish([(c, scalar, nc.sync) for c in chunks], span(HALF, HALF))
-            warm_up(cos_psum, 1)
+        finish([(c, scalar, nc.sync) for c in range(CHUNKS)], span(HALF, HALF))
         finish([(0, scalar, nc.sync)], quarters[0])
         finish([(1, vector, nc.sync), (2, scalar, nc.sync), (3, vector, nc.sync)], lower)
         finish([(0, scalar, nc.scalar)], quarters[1])

from contextlib import ExitStack

import concourse.masks as masks
import concourse.mybir as mybir

BF16 = mybir.dt.bfloat16
F32 = mybir.dt.float32
I32 = mybir.dt.int32
U32 = mybir.dt.uint32
U8 = mybir.dt.uint8
E4M3_X4 = mybir.dt.float8_e4m3fn_x4
E5M2_X4 = mybir.dt.float8_e5m2_x4
ALU = mybir.AluOpType

P = 128
PACK = 4
BATCH = 2
LENGTH = 256
WIDTH = 512
HALF = WIDTH // 2
LOWER = 0
UPPER = 1
ROWS = LENGTH // P
CHUNK = 128
CHUNKS = WIDTH // CHUNK
G_RUN = 4
RUN = 4

FLOPS = 2 * BATCH * LENGTH * WIDTH * WIDTH
BYTES = 2 * (2 * BATCH * LENGTH * WIDTH + 2 * LENGTH * WIDTH) + 4 * WIDTH * WIDTH


def span(first, count):
    return slice(first, first + count)


def tile_denseattentiononehead_pa_s_kernel(tc, hidden_states, W_q, cos, sin, grad_out, out):
    nc = tc.nc

    x_rows = hidden_states.rearrange("b (p i) w -> i p b w", i=ROWS)
    cos_rows = cos.rearrange("(p i) w -> i p w", i=ROWS)
    sin_rows = sin.rearrange("(p i) w -> p i w", i=ROWS)
    g_rows = grad_out.rearrange("b (p i) o -> b p i o", i=ROWS)

    with ExitStack() as ctx:
        keep = ctx.enter_context(tc.tile_pool(name="keep", bufs=1))
        results = ctx.enter_context(tc.tile_pool(name="results", bufs=10))
        psum = ctx.enter_context(tc.psum_pool(name="psum", bufs=5))
        tables = ctx.enter_context(tc.psum_pool(name="tables", bufs=1))
        ctx.enter_context(tc.manual_schedule())

        x_sb = keep.tile([P, BATCH, ROWS, WIDTH], BF16)
        cos_sb = keep.tile([P, ROWS, WIDTH], BF16)
        sin_sb = keep.tile([P, ROWS, WIDTH], BF16)
        g_sb = keep.tile([P, BATCH, ROWS, WIDTH], BF16)

        h_codes = keep.tile([P, 2 * WIDTH], U32, align_bytes=64)
        h_scales = keep.tile([P, 2 * WIDTH], U8, align_bytes=64)
        nc.vector.memset(h_codes[:, WIDTH:].bitcast(I32), 0)
        nc.vector.memset(h_scales[:, WIDTH:].bitcast(I32), 0)

        first_in = keep.tile([P, 1], F32)
        first_out = keep.tile([P, 1], F32)
        nc.vector.memset(first_in[:], 0.0)
        nc.scalar.copy(out=first_out[:], in_=first_in[:])

        identity = keep.tile([P, P], BF16)
        masks.make_identity(nc, identity[:])

        both, first, last = span(0, BATCH), span(0, 1), span(1, 1)
        every, upper, lower = span(0, WIDTH), span(HALF, HALF), span(0, HALF)

        def load_x(i, b):
            nc.sync.dma_start(out=x_sb[:, b, i, :], in_=x_rows[i, :, b, :])

        def load_cos(i, cols):
            nc.sync.dma_start(out=cos_sb[:, i, cols], in_=cos_rows[i, :, cols])

        def load_g(b, cols):
            nc.sync.dma_start(out=g_sb[:, b, :, cols], in_=g_rows[b, :, :, cols])

        load_x(0, 0)
        load_cos(0, upper)
        load_cos(0, lower)
        load_x(0, 1)
        nc.sync.dma_start(out=sin_sb[:], in_=sin_rows)
        load_cos(1, every)
        load_x(1, 0)
        load_g(0, span(0, CHUNK))
        load_x(1, 1)
        load_g(1, span(0, CHUNK))
        for cols in (span(CHUNK, CHUNK), upper):
            for b in range(BATCH):
                load_g(b, cols)

        cos_psum = tables.tile([P, WIDTH], F32)
        sin_psum = tables.tile([P, HALF], F32)

        g_grouped = keep.tile([P, WIDTH, PACK], BF16, align_bytes=64)
        g_codes = keep.tile([P, WIDTH + CHUNK], U32, align_bytes=64)
        g_scales = keep.tile([P, WIDTH + CHUNK], U8, align_bytes=64)
        nc.vector.memset(g_codes[:, WIDTH:].bitcast(I32), 0)
        nc.vector.memset(g_scales[:, WIDTH:].bitcast(I32), 0)
        for c in range(CHUNKS):
            cols = span(c * CHUNK, CHUNK)
            nc.scalar.copy(
                out=g_grouped[:, cols, :].rearrange("p (c r) t -> p c t r", r=G_RUN),
                in_=g_sb[:, :, :, cols].rearrange("p b i (c r) -> p c (b i) r", r=G_RUN),
            )

        def quantise_g(cols):
            nc.vector.quantize_mx(
                out=g_codes[:, cols].bitcast(E5M2_X4),
                scales=g_scales[:, cols],
                in_=g_grouped[:, cols, :].rearrange("p o t -> p (o t)"),
            )

        x_cos = keep.tile([P, BATCH, ROWS, WIDTH], F32)
        x_sin = keep.tile([P, BATCH, ROWS, WIDTH], F32)
        h_grouped = keep.tile([P, WIDTH, PACK], BF16, align_bytes=64)

        def multiply(out, x, table, engine=nc.vector):
            engine.tensor_tensor(
                out=out, in0=x, in1=table.unsqueeze(1).to_broadcast(x.shape), op=ALU.mult
            )

        def multiply_by_cos(i, batches, cols):
            table = cos_psum[:, cols] if i == 1 else cos_sb[:, i, cols]
            multiply(x_cos[:, batches, i, cols], x_sb[:, batches, i, cols], table)

        def multiply_by_sin(i, batches, half, engine=nc.vector):
            table = sin_psum[:] if i == 1 and half == UPPER else sin_sb[:, i, span(half * HALF, HALF)]
            multiply(
                x_sin[:, batches, i, span(half * HALF, HALF)],
                x_sb[:, batches, i, span((1 - half) * HALF, HALF)],
                table,
                engine,
            )

        def multiply_both_halves_by_sin(i):
            x = x_sb[:, :, i, :].rearrange("p b (h w) -> p b h w", w=HALF)[:, :, ::-1, :]
            table = sin_sb[:, i, :].rearrange("p (h w) -> p h w", w=HALF)
            multiply(x_sin[:, :, i, :].rearrange("p b (h w) -> p b h w", w=HALF), x, table)

        def add_terms(half, cols):
            nc.vector.tensor_tensor(
                out=h_grouped[:, cols, :].rearrange("p (c r) t -> p c t r", r=RUN),
                in0=x_cos[:, :, :, cols].rearrange("p b i (c r) -> p c (b i) r", r=RUN),
                in1=x_sin[:, :, :, cols].rearrange("p b i (c r) -> p c (b i) r", r=RUN),
                op=ALU.add if half == UPPER else ALU.subtract,
            )

        def quantise_h(cols):
            nc.vector.quantize_mx(
                out=h_codes[:, cols].bitcast(E4M3_X4),
                scales=h_scales[:, cols],
                in_=h_grouped[:, cols, :].rearrange("p j t -> p (j t)"),
            )

        def finish(chunks, js):
            window = span(js.start, WIDTH)
            width = js.stop - js.start
            for c, copy, queue in chunks:
                cols = span(c * CHUNK, CHUNK)
                acc = psum.tile([CHUNK, WIDTH], F32)
                nc.tensor.matmul_mx(
                    out=acc[:],
                    lhsT=g_codes[:, cols].bitcast(E5M2_X4),
                    lhsT_scale=g_scales[:, cols],
                    rhs=h_codes[:, window].bitcast(E4M3_X4),
                    rhs_scale=h_scales[:, window],
                    start=True,
                    stop=True,
                )
                result = results.tile([CHUNK, width], F32)
                copy(out=result[:], in_=acc[:, :width])
                queue.dma_start(out=out[cols, js], in_=result[:])

        def warm_up(count):
            acc = psum.tile([CHUNK, WIDTH], F32)
            for n in range(count):
                nc.tensor.matmul_mx(
                    out=acc[:],
                    lhsT=g_codes[:, WIDTH:].bitcast(E5M2_X4),
                    lhsT_scale=g_scales[:, WIDTH:],
                    rhs=h_codes[:, WIDTH:].bitcast(E4M3_X4),
                    rhs_scale=h_scales[:, WIDTH:],
                    start=n == 0,
                    stop=n == count - 1,
                )

        warm_up(3)

        nc.tensor.matmul(out=cos_psum[:], lhsT=identity[:], rhs=cos_sb[:, 1, :], start=True, stop=True)
        nc.tensor.matmul(out=sin_psum[:], lhsT=identity[:], rhs=sin_sb[:, 1, HALF:], start=True, stop=True)

        warm_up(10)

        multiply_by_cos(0, first, upper)
        multiply_by_cos(0, first, lower)
        multiply_by_cos(0, last, every)
        multiply_both_halves_by_sin(0)
        multiply_by_cos(1, first, every)
        multiply_by_cos(1, last, upper)
        multiply_by_sin(1, both, UPPER)
        multiply_by_cos(1, last, lower)
        multiply_by_sin(1, both, LOWER, nc.gpsimd)
        add_terms(UPPER, span(HALF, HALF))
        quantise_g(span(0, HALF))
        quantise_h(span(HALF, HALF))
        quarters = [span(q * HALF // 2, HALF // 2) for q in (1, 0)]
        add_terms(LOWER, quarters[0])
        quantise_g(span(HALF, HALF))
        add_terms(LOWER, quarters[1])
        for cols in quarters:
            quantise_h(cols)

        vector, scalar = nc.vector.tensor_copy, nc.scalar.copy
        finish([(c, scalar, nc.sync) for c in range(CHUNKS)], span(HALF, HALF))
        finish([(0, scalar, nc.sync)], quarters[0])
        finish([(1, vector, nc.sync), (2, scalar, nc.sync), (3, vector, nc.sync)], lower)
        finish([(0, scalar, nc.scalar)], quarters[1])
